import numpy as np
import ml_dtypes


def mxq(x, axis, fmt="e4m3"):
    dtype, down = {"e4m3": (ml_dtypes.float8_e4m3fn, 7), "e5m2": (ml_dtypes.float8_e5m2, 14)}[fmt]
    v = np.moveaxis(np.asarray(x, np.float32).astype(ml_dtypes.bfloat16).astype(np.float64), axis, -1)
    blocks = v.reshape(v.shape[:-1] + (-1, 32))
    amax = np.abs(blocks).max(-1, keepdims=True)
    byte = np.maximum(np.where(amax > 0, np.frexp(amax)[1] - 1 + 127, 0) - down, 1)
    scale = np.exp2(byte - 127.0)
    codes = (blocks / scale).astype(np.float32).astype(dtype).astype(np.float64)
    return np.moveaxis((codes * scale).reshape(v.shape), -1, axis)


WIDE = False


def mx_kscale(k):
    if not WIDE:
        return np.ones(k)
    levels = np.array([10, -10, 5, -5, 0])
    a = np.random.permutation(np.resize(levels, k // 512 * 4)).reshape(k // 512, 4)
    idx = np.arange(k)
    return np.exp2(a[idx // 512, idx % 128 // 32])


BF16 = ml_dtypes.bfloat16


def bf(x):
    return np.asarray(x, np.float32).astype(BF16)


def f64(x):
    return np.asarray(x).astype(np.float64)


E2M1 = np.array([0.0, 0.5, 1.0, 1.5, 2.0, 3.0, 4.0, 6.0, -0.0, -0.5, -1.0, -1.5, -2.0, -3.0, -4.0, -6.0])


def pack_weight(w, fmt):
    k, n = w.shape
    w = f64(bf(w)).reshape(k // 32, 32, n)
    amax = np.abs(w).max(1)
    if fmt == "e4m3":
        byte = np.frexp(amax)[1] - 1 + 127 - 7
    else:
        mant, ex = np.frexp(amax / 6.0)
        byte = np.where(mant > 0.5, ex, ex - 1) + 127
    byte = np.clip(np.where(amax > 0, byte, 1), 1, 254)
    scaled = (w * np.exp2(127.0 - byte)[:, None, :]).reshape(k, n).astype(np.float32)
    by_word = np.ascontiguousarray(scaled.reshape(k // 512, 128, 4, n).transpose(0, 1, 3, 2))
    if fmt == "e4m3":
        words = by_word.astype(ml_dtypes.float8_e4m3fn).view(np.uint8)
    else:
        c = by_word.astype(ml_dtypes.float4_e2m1fn).view(np.uint8) & 0xF
        words = c[..., 0::2] | (c[..., 1::2] << 4)
    return np.ascontiguousarray(words), np.ascontiguousarray(byte.astype(np.uint8).reshape(k // 512, 16, n))


def unpack_weight(words, scales, fmt):
    g, p, n, _ = words.shape
    if fmt == "e4m3":
        vals = np.ascontiguousarray(words).view(ml_dtypes.float8_e4m3fn).astype(np.float64)
    else:
        nib = np.empty((g, p, n, 4), np.uint8)
        nib[..., 0::2] = words & 0xF
        nib[..., 1::2] = words >> 4
        vals = E2M1[nib]
    vals = vals * np.repeat(np.exp2(scales.astype(np.float64) - 127.0), 8, axis=1)[..., None]
    return vals.transpose(0, 1, 3, 2).reshape(g * 512, n)

def pack4(w):
    words, scales = pack_weight(w, "e2m1")
    return words.reshape(words.shape[0], 128, -1), scales


def unpack4(words, scales):
    return unpack_weight(words.reshape(words.shape[0], 128, -1, 2), scales, "e2m1")


B, G, DB, DR = 128, 16, 1024, 2048


def mish(v):
    return v * np.tanh(np.log(1.0 + np.exp(v)))


def setup_inputs():
    s, t = mx_kscale(DR), mx_kscale(DB)
    BB_feature = bf(np.random.standard_normal((B, G, DB)) * t)
    RF_feature = bf(np.random.standard_normal((B, DR)) * s)
    W_rfrf = np.random.standard_normal((DR, DR)) / np.sqrt(DR) / s
    W_rfrf_words, W_rfrf_scales = pack4(np.ascontiguousarray(W_rfrf.T))
    b_rfrf = bf(np.random.standard_normal(DR) * 0.5)
    W_bbrf = np.random.standard_normal((DR, DB)) * np.sqrt(G / DB) / t
    W_bbrf_words, W_bbrf_scales = pack4(np.ascontiguousarray(W_bbrf.T))
    b_bbrf = bf(np.random.standard_normal(DR) * 0.5)
    return {"BB_feature": BB_feature,
            "RF_feature": RF_feature,
            "W_rfrf_words": W_rfrf_words,
            "W_rfrf_scales": W_rfrf_scales,
            "b_rfrf": b_rfrf,
            "W_bbrf_words": W_bbrf_words,
            "W_bbrf_scales": W_bbrf_scales,
            "b_bbrf": b_bbrf}


def reference(BB_feature, RF_feature, W_rfrf_words, W_rfrf_scales, b_rfrf, W_bbrf_words, W_bbrf_scales, b_bbrf):
    BB_mean = np.mean(f64(BB_feature), axis=-2)
    RF_to_RF = mish((mxq(f64(RF_feature), 1, "e4m3") @ unpack4(W_rfrf_words, W_rfrf_scales)) + f64(b_rfrf))
    BB_to_RF = mish((mxq(BB_mean, 1, "e4m3") @ unpack4(W_bbrf_words, W_bbrf_scales)) + f64(b_bbrf))
    return RF_to_RF + BB_to_RF

@@ -1,0 +1,242 @@
+from contextlib import ExitStack
+
+import concourse.mybir as mybir
+from concourse.masks import make_identity
+
+F32 = mybir.dt.float32
+BF16 = mybir.dt.bfloat16
+I32 = mybir.dt.int32
+U32 = mybir.dt.uint32
+U8 = mybir.dt.uint8
+FP8X4 = mybir.dt.float8_e4m3fn_x4
+FP4X4 = mybir.dt.float4_e2m1fn_x4
+ACT = mybir.ActivationFunctionType
+ALU = mybir.AluOpType
+AXIS = mybir.AxisListType
+
+P = 128
+PACK = 4
+K_PASS = P * PACK
+GROUPS = 16
+DB = 1024
+DR = 2048
+N_TILE = 512
+N_TILES = DR // N_TILE
+RF_PASSES = DR // K_PASS
+BB_PASSES = DB // K_PASS
+SAMPLES_PER_TILE = P // GROUPS
+BB_TILES = P // SAMPLES_PER_TILE
+BB_TILES_PER_DMA = 2
+K_CHUNKS = DB // P
+EXP_CAP = 2.0**60
+
+FLOPS = 2 * P * DR * DR + 2 * P * DB * DR
+
+
+def load_scale_planes(nc, planes, scales, passes_per_dma):
+    words = scales.bitcast(I32)
+    passes = scales.shape[0]
+    for first in range(0, passes, passes_per_dma):
+        some = slice(first, first + passes_per_dma)
+        for quadrant in range(2):
+            for r in range(4):
+                nc.sync.dma_start(
+                    out=planes[32 * quadrant + r : P : 64, some, :].bitcast(I32),
+                    in_=words[some, 4 * quadrant + r : 16 : 8, :].rearrange("g q n -> q g n"),
+                )
+
+
+def tile_gnn_layer_pa_kernel(
+    tc,
+    BB_feature,
+    RF_feature,
+    W_rfrf_words,
+    W_rfrf_scales,
+    b_rfrf,
+    W_bbrf_words,
+    W_bbrf_scales,
+    b_bbrf,
+    out,
+):
+    nc = tc.nc
+    with ExitStack() as ctx:
+        keep = ctx.enter_context(tc.tile_pool(name="keep", bufs=1))
+        psum_main = ctx.enter_context(tc.psum_pool(name="psum_main", bufs=4))
+        psum_side = ctx.enter_context(tc.psum_pool(name="psum_side", bufs=2))
+        ctx.enter_context(tc.manual_schedule())
+
+        rf_sb = keep.tile([P, DR], BF16, name="rf_sb")
+        bb_sb = keep.tile([P, BB_TILES, DB], BF16, name="bb_sb")
+        wrf_words = keep.tile([P, RF_PASSES, 2 * DR], U8, name="wrf_words", align_bytes=64)
+        wbb_words = keep.tile([P, BB_PASSES, 2 * DR], U8, name="wbb_words", align_bytes=64)
+        wrf_planes = keep.tile([P, RF_PASSES, DR], U8, name="wrf_planes", align_bytes=64)
+        wbb_planes = keep.tile([P, BB_PASSES, DR], U8, name="wbb_planes", align_bytes=64)
+        bias_rows = keep.tile([P, P], BF16, name="bias_rows")
+
+        nc.vector.memset(bias_rows[:], 0.0)
+        nc.vector.memset(wrf_planes[:].rearrange("p g n -> p (g n)").bitcast(I32), 0)
+        nc.vector.memset(wbb_planes[:].rearrange("p g n -> p (g n)").bitcast(I32), 0)
+        ident_f32 = keep.tile([P, P], F32, name="ident_f32")
+        make_identity(nc, ident_f32[:])
+        ident_bf = keep.tile([P, P], BF16, name="ident_bf")
+        nc.vector.tensor_copy(out=ident_bf[:], in_=ident_f32[:])
+        group_sum = keep.tile([P, SAMPLES_PER_TILE], F32, name="group_sum")
+        nc.vector.tensor_reduce(
+            out=group_sum[:],
+            in_=ident_f32[:].rearrange("p (i r) -> p i r", r=GROUPS),
+            axis=AXIS.X,
+            op=ALU.add,
+        )
+        group_mean = keep.tile([P, SAMPLES_PER_TILE], BF16, name="group_mean")
+        nc.vector.tensor_scalar_mul(out=group_mean[:], in0=group_sum[:], scalar1=1.0 / GROUPS)
+
+        bias_chunks = DR // P
+        nc.scalar.dma_start(out=bias_rows[0:bias_chunks, :], in_=b_rfrf.rearrange("(r c) -> r c", c=P))
+        nc.scalar.dma_start(
+            out=bias_rows[bias_chunks : 2 * bias_chunks, :], in_=b_bbrf.rearrange("(r c) -> r c", c=P)
+        )
+        nc.sync.dma_start(out=rf_sb[:], in_=RF_feature)
+        load_scale_planes(nc, wrf_planes, W_rfrf_scales, passes_per_dma=2)
+        for g in range(RF_PASSES):
+            nc.sync.dma_start(out=wrf_words[:, g, :].bitcast(I32), in_=W_rfrf_words[g].bitcast(I32))
+        bb_rows = BB_feature.rearrange("b g k -> (b g) k")
+        for first in range(0, BB_TILES, BB_TILES_PER_DMA):
+            nc.sync.dma_start(
+                out=bb_sb[:, first : first + BB_TILES_PER_DMA, :],
+                in_=bb_rows[first * P : (first + BB_TILES_PER_DMA) * P, :].rearrange("(j p) k -> p j k", p=P),
+            )
+        load_scale_planes(nc, wbb_planes, W_bbrf_scales, passes_per_dma=2)
+        for g in range(BB_PASSES):
+            nc.sync.dma_start(out=wbb_words[:, g, :].bitcast(I32), in_=W_bbrf_words[g].bitcast(I32))
+
+        bias_cols_ps = psum_side.tile([P, P], BF16, name="bias_cols_ps", tag="side")
+        nc.tensor.transpose(bias_cols_ps[:], bias_rows[:], ident_bf[:])
+        bias_cols = keep.tile([P, 2 * bias_chunks], BF16, name="bias_cols")
+        nc.vector.tensor_copy(out=bias_cols[:], in_=bias_cols_ps[:, 0 : 2 * bias_chunks])
+        bias_all = keep.tile([P, 2 * DR], BF16, name="bias_all")
+        chunks_per_bank = 8
+        for bank in range(2 * bias_chunks // chunks_per_bank):
+            spread_ps = psum_main.tile([P, chunks_per_bank * P], BF16, name="spread_ps", tag="main")
+            for i in range(chunks_per_bank):
+                j = bank * chunks_per_bank + i
+                nc.tensor.transpose(
+                    spread_ps[:, i * P : (i + 1) * P], bias_cols[:, j : j + 1].to_broadcast([P, P]), ident_bf[:]
+                )
+            cols = slice(bank * chunks_per_bank * P, (bank + 1) * chunks_per_bank * P)
+            if bank % 2 == 0:
+                nc.scalar.copy(out=bias_all[:, cols], in_=spread_ps[:])
+            else:
+                nc.vector.tensor_copy(out=bias_all[:, cols], in_=spread_ps[:])
+
+        rf_words = rf_sb[:].bitcast(F32)
+        rf_grouped = keep.tile([P, RF_PASSES, P, PACK], BF16, name="rf_grouped", align_bytes=64)
+        rf_grouped_words = rf_grouped[:].bitcast(F32)
+        for half in range(2):
+            rf_t_ps = psum_side.tile([P, 2, 2, P], F32, name="rf_t_ps", tag="side")
+            for g_in in range(2):
+                g = 2 * half + g_in
+                for u in range(2):
+                    nc.tensor.transpose(
+                        rf_t_ps[:, g_in, u, :],
+                        rf_words[:, g * K_PASS // 2 + u : (g + 1) * K_PASS // 2 : 2],
+                        ident_f32[:],
+                    )
+            dst = rf_grouped_words[:, 2 * half : 2 * half + 2, :, :]
+            src = rf_t_ps[:].rearrange("p g u b -> p g b u")
+            if half == 0:
+                nc.vector.tensor_copy(out=dst, in_=src)
+            else:
+                nc.scalar.copy(out=dst, in_=src)
+        rf_codes = keep.tile([P, RF_PASSES, P], U32, name="rf_codes", align_bytes=64)
+        rf_scales = keep.tile([P, RF_PASSES, P], U8, name="rf_scales", align_bytes=64)
+        nc.vector.quantize_mx(
+            out=rf_codes[:].rearrange("p g b -> p (g b)").bitcast(FP8X4),
+            scales=rf_scales[:].rearrange("p g b -> p (g b)"),
+            in_=rf_grouped[:].rearrange("p g b t -> p (g b t)"),
+        )
+
+        def product(x_codes, x_scales, w_words, w_planes, passes, name):
+            banks = []
+            for c in range(N_TILES):
+                banks.append(psum_main.tile([P, N_TILE], F32, name="%s_%d" % (name, c), tag="main"))
+            for g in range(passes):
+                for c in range(N_TILES):
+                    nc.tensor.matmul_mx(
+                        out=banks[c][:],
+                        lhsT=x_codes[:, g, :].bitcast(FP8X4),
+                        lhsT_scale=x_scales[:, g, :],
+                        rhs=w_words[:, g, 2 * c * N_TILE : 2 * (c + 1) * N_TILE].bitcast(FP4X4),
+                        rhs_scale=w_planes[:, g, c * N_TILE : (c + 1) * N_TILE],
+                        start=(g == 0),
+                        stop=(g == passes - 1),
+                    )
+            return banks
+
+        def add_bias_and_exp(banks, bias, z, w):
+            for c in range(N_TILES):
+                cols = slice(c * N_TILE, (c + 1) * N_TILE)
+                nc.vector.tensor_tensor(out=z[:, cols], in0=banks[c][:], in1=bias[:, cols], op=ALU.add)
+                nc.scalar.activation(out=w[:, cols], in_=z[:, cols], func=ACT.Exp)
+            nc.vector.tensor_scalar_min(out=w[:], in0=w[:], scalar1=EXP_CAP)
+
+        z_rf = keep.tile([P, DR], F32, name="z_rf")
+        w_rf = keep.tile([P, DR], F32, name="w_rf")
+        rf_banks = product(rf_codes, rf_scales, wrf_words, wrf_planes, RF_PASSES, "rf_acc")
+        add_bias_and_exp(rf_banks, bias_all[:, 0:DR], z_rf, w_rf)
+        nc.scalar.activation(out=w_rf[:], in_=w_rf[:], func=ACT.Ln, bias=1.0)
+        nc.scalar.activation(out=w_rf[:], in_=w_rf[:], func=ACT.Tanh)
+
+        mean_t_ps = []
+        for g in range(BB_PASSES):
+            mean_t_ps.append(psum_side.tile([P, PACK, P], F32, name="mean_t_ps_%d" % g, tag="side"))
+        for j in range(BB_TILES):
+            for c in range(K_CHUNKS):
+                nc.tensor.matmul(
+                    out=mean_t_ps[c // PACK][:, c % PACK, j * SAMPLES_PER_TILE : (j + 1) * SAMPLES_PER_TILE],
+                    lhsT=bb_sb[:, j, c * P : (c + 1) * P],
+                    rhs=group_mean[:],
+                    start=True,
+                    stop=True,
+                )
+        mean_t = keep.tile([P, BB_PASSES, PACK, P], BF16, name="mean_t")
+        nc.vector.tensor_copy(out=mean_t[:, 0], in_=mean_t_ps[0][:])
+        nc.scalar.copy(out=mean_t[:, 1], in_=mean_t_ps[1][:])
+        mean_sb = keep.tile([P, BB_PASSES, K_PASS], BF16, name="mean_sb")
+        for g in range(BB_PASSES):
+            mean_ps = psum_main.tile([P, PACK, P], BF16, name="mean_ps", tag="main")
+            for c in range(PACK):
+                nc.tensor.transpose(mean_ps[:, c, :], mean_t[:, g, c, :], ident_bf[:])
+            if g == 0:
+                nc.vector.tensor_copy(out=mean_sb[:, g, :], in_=mean_ps[:].rearrange("b c m -> b (c m)"))
+            else:
+                nc.scalar.copy(out=mean_sb[:, g, :], in_=mean_ps[:].rearrange("b c m -> b (c m)"))
+        bb_grouped = keep.tile([P, BB_PASSES, P, PACK], BF16, name="bb_grouped", align_bytes=64)
+        bb_codes = keep.tile([P, BB_PASSES, P], U32, name="bb_codes", align_bytes=64)
+        bb_scales = keep.tile([P, BB_PASSES, P], U8, name="bb_scales", align_bytes=64)
+        for g in range(BB_PASSES):
+            bb_t_ps = psum_main.tile([P, PACK, P], BF16, name="bb_t_ps", tag="main")
+            for t in range(PACK):
+                nc.tensor.transpose(bb_t_ps[:, t, :], mean_sb[:, g, t:K_PASS:PACK], ident_bf[:])
+            if g == 0:
+                nc.vector.tensor_copy(out=bb_grouped[:, g], in_=bb_t_ps[:].rearrange("p t b -> p b t"))
+            else:
+                nc.scalar.copy(out=bb_grouped[:, g], in_=bb_t_ps[:].rearrange("p t b -> p b t"))
+        for g in range(BB_PASSES):
+            nc.vector.quantize_mx(
+                out=bb_codes[:, g, :].bitcast(FP8X4),
+                scales=bb_scales[:, g, :],
+                in_=bb_grouped[:, g].rearrange("p b t -> p (b t)"),
+            )
+
+        z_bb = keep.tile([P, DR], F32, name="z_bb")
+        w_bb = keep.tile([P, DR], F32, name="w_bb")
+        bb_banks = product(bb_codes, bb_scales, wbb_words, wbb_planes, BB_PASSES, "bb_acc")
+        add_bias_and_exp(bb_banks, bias_all[:, DR : 2 * DR], z_bb, w_bb)
+        nc.vector.tensor_tensor(out=w_rf[:], in0=w_rf[:], in1=z_rf[:], op=ALU.mult)
+        nc.scalar.activation(out=w_bb[:], in_=w_bb[:], func=ACT.Ln, bias=1.0)
+        for c in range(N_TILES):
+            cols = slice(c * N_TILE, (c + 1) * N_TILE)
+            nc.scalar.activation(out=w_bb[:, cols], in_=w_bb[:, cols], func=ACT.Tanh)
+            nc.vector.tensor_tensor(out=w_bb[:, cols], in0=w_bb[:, cols], in1=z_bb[:, cols], op=ALU.mult)
+            nc.vector.tensor_tensor(out=w_bb[:, cols], in0=w_bb[:, cols], in1=w_rf[:, cols], op=ALU.add)
+            nc.sync.dma_start(out=out[:, cols], in_=w_bb[:, cols])

@@ -24,26 +24,22 @@ N_TILE = 512
 N_TILES = DR // N_TILE
 RF_PASSES = DR // K_PASS
 BB_PASSES = DB // K_PASS
-SAMPLES_PER_TILE = P // GROUPS
+GROUPS_PER_ROW = 2
+SAMPLES_PER_TILE = P * GROUPS_PER_ROW // GROUPS
 BB_TILES = P // SAMPLES_PER_TILE
-BB_TILES_PER_DMA = 2
 K_CHUNKS = DB // P
 EXP_CAP = 2.0**60
 
 FLOPS = 2 * P * DR * DR + 2 * P * DB * DR
 
 
-def load_scale_planes(nc, planes, scales, passes_per_dma):
+def load_scale_planes(nc, planes, scales):
     words = scales.bitcast(I32)
-    passes = scales.shape[0]
-    for first in range(0, passes, passes_per_dma):
-        some = slice(first, first + passes_per_dma)
-        for quadrant in range(2):
-            for r in range(4):
-                nc.sync.dma_start(
-                    out=planes[32 * quadrant + r : P : 64, some, :].bitcast(I32),
-                    in_=words[some, 4 * quadrant + r : 16 : 8, :].rearrange("g q n -> q g n"),
-                )
+    for r in range(4):
+        nc.sync.dma_start(
+            out=planes[r:P:32, :, :].bitcast(I32),
+            in_=words[:, r:16:4, :].rearrange("g q n -> q g n"),
+        )
 
 
 def tile_gnn_layer_pa_kernel(
@@ -66,7 +62,7 @@ def tile_gnn_layer_pa_kernel(
         ctx.enter_context(tc.manual_schedule())
 
         rf_sb = keep.tile([P, DR], BF16, name="rf_sb")
-        bb_sb = keep.tile([P, BB_TILES, DB], BF16, name="bb_sb")
+        bb_sb = keep.tile([P, BB_TILES, GROUPS_PER_ROW, DB], BF16, name="bb_sb")
         wrf_words = keep.tile([P, RF_PASSES, 2 * DR], U8, name="wrf_words", align_bytes=64)
         wbb_words = keep.tile([P, BB_PASSES, 2 * DR], U8, name="wbb_words", align_bytes=64)
         wrf_planes = keep.tile([P, RF_PASSES, DR], U8, name="wrf_planes", align_bytes=64)
@@ -83,7 +79,7 @@ def tile_gnn_layer_pa_kernel(
         group_sum = keep.tile([P, SAMPLES_PER_TILE], F32, name="group_sum")
         nc.vector.tensor_reduce(
             out=group_sum[:],
-            in_=ident_f32[:].rearrange("p (i r) -> p i r", r=GROUPS),
+            in_=ident_f32[:].rearrange("p (i r) -> p i r", i=SAMPLES_PER_TILE),
             axis=AXIS.X,
             op=ALU.add,
         )
@@ -96,18 +92,17 @@ def tile_gnn_layer_pa_kernel(
             out=bias_rows[bias_chunks : 2 * bias_chunks, :], in_=b_bbrf.rearrange("(r c) -> r c", c=P)
         )
         nc.sync.dma_start(out=rf_sb[:], in_=RF_feature)
-        load_scale_planes(nc, wrf_planes, W_rfrf_scales, passes_per_dma=2)
         for g in range(RF_PASSES):
             nc.sync.dma_start(out=wrf_words[:, g, :].bitcast(I32), in_=W_rfrf_words[g].bitcast(I32))
-        bb_rows = BB_feature.rearrange("b g k -> (b g) k")
-        for first in range(0, BB_TILES, BB_TILES_PER_DMA):
+        load_scale_planes(nc, wrf_planes, W_rfrf_scales)
+        bb_rows = BB_feature.rearrange("b (h i) k -> (b h) (i k)", i=GROUPS_PER_ROW)
+        for j in range(BB_TILES):
             nc.sync.dma_start(
-                out=bb_sb[:, first : first + BB_TILES_PER_DMA, :],
-                in_=bb_rows[first * P : (first + BB_TILES_PER_DMA) * P, :].rearrange("(j p) k -> p j k", p=P),
+                out=bb_sb[:, j].rearrange("p i k -> p (i k)"), in_=bb_rows[j * P : (j + 1) * P, :]
             )
-        load_scale_planes(nc, wbb_planes, W_bbrf_scales, passes_per_dma=2)
         for g in range(BB_PASSES):
             nc.sync.dma_start(out=wbb_words[:, g, :].bitcast(I32), in_=W_bbrf_words[g].bitcast(I32))
+        load_scale_planes(nc, wbb_planes, W_bbrf_scales)
 
         bias_cols_ps = psum_side.tile([P, P], BF16, name="bias_cols_ps", tag="side")
         nc.tensor.transpose(bias_cols_ps[:], bias_rows[:], ident_bf[:])
@@ -159,8 +154,8 @@ def tile_gnn_layer_pa_kernel(
             banks = []
             for c in range(N_TILES):
                 banks.append(psum_main.tile([P, N_TILE], F32, name="%s_%d" % (name, c), tag="main"))
-            for g in range(passes):
-                for c in range(N_TILES):
+            for c in range(N_TILES):
+                for g in range(passes):
                     nc.tensor.matmul_mx(
                         out=banks[c][:],
                         lhsT=x_codes[:, g, :].bitcast(FP8X4),
@@ -191,13 +186,14 @@ def tile_gnn_layer_pa_kernel(
             mean_t_ps.append(psum_side.tile([P, PACK, P], F32, name="mean_t_ps_%d" % g, tag="side"))
         for j in range(BB_TILES):
             for c in range(K_CHUNKS):
-                nc.tensor.matmul(
-                    out=mean_t_ps[c // PACK][:, c % PACK, j * SAMPLES_PER_TILE : (j + 1) * SAMPLES_PER_TILE],
-                    lhsT=bb_sb[:, j, c * P : (c + 1) * P],
-                    rhs=group_mean[:],
-                    start=True,
-                    stop=True,
-                )
+                for i in range(GROUPS_PER_ROW):
+                    nc.tensor.matmul(
+                        out=mean_t_ps[c // PACK][:, c % PACK, j * SAMPLES_PER_TILE : (j + 1) * SAMPLES_PER_TILE],
+                        lhsT=bb_sb[:, j, i, c * P : (c + 1) * P],
+                        rhs=group_mean[:],
+                        start=(i == 0),
+                        stop=(i == GROUPS_PER_ROW - 1),
+                    )
         mean_t = keep.tile([P, BB_PASSES, PACK, P], BF16, name="mean_t")
         nc.vector.tensor_copy(out=mean_t[:, 0], in_=mean_t_ps[0][:])
         nc.scalar.copy(out=mean_t[:, 1], in_=mean_t_ps[1][:])

@@ -87,22 +87,22 @@ def tile_gnn_layer_pa_kernel(
         nc.vector.tensor_scalar_mul(out=group_mean[:], in0=group_sum[:], scalar1=1.0 / GROUPS)
 
         bias_chunks = DR // P
-        nc.scalar.dma_start(out=bias_rows[0:bias_chunks, :], in_=b_rfrf.rearrange("(r c) -> r c", c=P))
-        nc.scalar.dma_start(
+        nc.sync.dma_start(out=bias_rows[0:bias_chunks, :], in_=b_rfrf.rearrange("(r c) -> r c", c=P))
+        nc.sync.dma_start(
             out=bias_rows[bias_chunks : 2 * bias_chunks, :], in_=b_bbrf.rearrange("(r c) -> r c", c=P)
         )
         nc.sync.dma_start(out=rf_sb[:], in_=RF_feature)
+        load_scale_planes(nc, wrf_planes, W_rfrf_scales)
         for g in range(RF_PASSES):
             nc.sync.dma_start(out=wrf_words[:, g, :].bitcast(I32), in_=W_rfrf_words[g].bitcast(I32))
-        load_scale_planes(nc, wrf_planes, W_rfrf_scales)
         bb_rows = BB_feature.rearrange("b (h i) k -> (b h) (i k)", i=GROUPS_PER_ROW)
         for j in range(BB_TILES):
             nc.sync.dma_start(
                 out=bb_sb[:, j].rearrange("p i k -> p (i k)"), in_=bb_rows[j * P : (j + 1) * P, :]
             )
+        load_scale_planes(nc, wbb_planes, W_bbrf_scales)
         for g in range(BB_PASSES):
             nc.sync.dma_start(out=wbb_words[:, g, :].bitcast(I32), in_=W_bbrf_words[g].bitcast(I32))
-        load_scale_planes(nc, wbb_planes, W_bbrf_scales)
 
         bias_cols_ps = psum_side.tile([P, P], BF16, name="bias_cols_ps", tag="side")
         nc.tensor.transpose(bias_cols_ps[:], bias_rows[:], ident_bf[:])
@@ -154,8 +154,8 @@ def tile_gnn_layer_pa_kernel(
             banks = []
             for c in range(N_TILES):
                 banks.append(psum_main.tile([P, N_TILE], F32, name="%s_%d" % (name, c), tag="main"))
-            for c in range(N_TILES):
-                for g in range(passes):
+            for g in range(passes):
+                for c in range(N_TILES):
                     nc.tensor.matmul_mx(
                         out=banks[c][:],
                         lhsT=x_codes[:, g, :].bitcast(FP8X4),
@@ -195,17 +195,14 @@ def tile_gnn_layer_pa_kernel(
                         stop=(i == GROUPS_PER_ROW - 1),
                     )
         mean_t = keep.tile([P, BB_PASSES, PACK, P], BF16, name="mean_t")
-        nc.vector.tensor_copy(out=mean_t[:, 0], in_=mean_t_ps[0][:])
-        nc.scalar.copy(out=mean_t[:, 1], in_=mean_t_ps[1][:])
+        for g in range(BB_PASSES):
+            nc.vector.tensor_copy(out=mean_t[:, g], in_=mean_t_ps[g][:])
         mean_sb = keep.tile([P, BB_PASSES, K_PASS], BF16, name="mean_sb")
         for g in range(BB_PASSES):
             mean_ps = psum_main.tile([P, PACK, P], BF16, name="mean_ps", tag="main")
             for c in range(PACK):
                 nc.tensor.transpose(mean_ps[:, c, :], mean_t[:, g, c, :], ident_bf[:])
-            if g == 0:
-                nc.vector.tensor_copy(out=mean_sb[:, g, :], in_=mean_ps[:].rearrange("b c m -> b (c m)"))
-            else:
-                nc.scalar.copy(out=mean_sb[:, g, :], in_=mean_ps[:].rearrange("b c m -> b (c m)"))
+            nc.vector.tensor_copy(out=mean_sb[:, g, :], in_=mean_ps[:].rearrange("b c m -> b (c m)"))
         bb_grouped = keep.tile([P, BB_PASSES, P, PACK], BF16, name="bb_grouped", align_bytes=64)
         bb_codes = keep.tile([P, BB_PASSES, P], U32, name="bb_codes", align_bytes=64)
         bb_scales = keep.tile([P, BB_PASSES, P], U8, name="bb_scales", align_bytes=64)
@@ -213,10 +210,7 @@ def tile_gnn_layer_pa_kernel(
             bb_t_ps = psum_main.tile([P, PACK, P], BF16, name="bb_t_ps", tag="main")
             for t in range(PACK):
                 nc.tensor.transpose(bb_t_ps[:, t, :], mean_sb[:, g, t:K_PASS:PACK], ident_bf[:])
-            if g == 0:
-                nc.vector.tensor_copy(out=bb_grouped[:, g], in_=bb_t_ps[:].rearrange("p t b -> p b t"))
-            else:
-                nc.scalar.copy(out=bb_grouped[:, g], in_=bb_t_ps[:].rearrange("p t b -> p b t"))
+            nc.vector.tensor_copy(out=bb_grouped[:, g], in_=bb_t_ps[:].rearrange("p t b -> p b t"))
         for g in range(BB_PASSES):
             nc.vector.quantize_mx(
                 out=bb_codes[:, g, :].bitcast(FP8X4),

@@ -76,6 +76,8 @@ def tile_gnn_layer_pa_kernel(
         make_identity(nc, ident_f32[:])
         ident_bf = keep.tile([P, P], BF16, name="ident_bf")
         nc.vector.tensor_copy(out=ident_bf[:], in_=ident_f32[:])
+        sort_k = keep.tile([P, PACK, P // PACK], BF16, name="sort_k")
+        nc.vector.tensor_copy(out=sort_k[:], in_=ident_f32[:].rearrange("p (i t) -> p t i", t=PACK))
         group_sum = keep.tile([P, SAMPLES_PER_TILE], F32, name="group_sum")
         nc.vector.tensor_reduce(
             out=group_sum[:],
@@ -172,7 +174,9 @@ def tile_gnn_layer_pa_kernel(
                 cols = slice(c * N_TILE, (c + 1) * N_TILE)
                 nc.vector.tensor_tensor(out=z[:, cols], in0=banks[c][:], in1=bias[:, cols], op=ALU.add)
                 nc.scalar.activation(out=w[:, cols], in_=z[:, cols], func=ACT.Exp)
-            nc.vector.tensor_scalar_min(out=w[:], in0=w[:], scalar1=EXP_CAP)
+            for c in range(N_TILES):
+                cols = slice(c * N_TILE, (c + 1) * N_TILE)
+                nc.vector.tensor_scalar_min(out=w[:, cols], in0=w[:, cols], scalar1=EXP_CAP)
 
         z_rf = keep.tile([P, DR], F32, name="z_rf")
         w_rf = keep.tile([P, DR], F32, name="w_rf")
@@ -197,19 +201,24 @@ def tile_gnn_layer_pa_kernel(
         mean_t = keep.tile([P, BB_PASSES, PACK, P], BF16, name="mean_t")
         for g in range(BB_PASSES):
             nc.vector.tensor_copy(out=mean_t[:, g], in_=mean_t_ps[g][:])
-        mean_sb = keep.tile([P, BB_PASSES, K_PASS], BF16, name="mean_sb")
+        quarter = P // PACK
+        mean_sb = keep.tile([P, BB_PASSES, PACK, P], BF16, name="mean_sb")
         for g in range(BB_PASSES):
             mean_ps = psum_main.tile([P, PACK, P], BF16, name="mean_ps", tag="main")
             for c in range(PACK):
-                nc.tensor.transpose(mean_ps[:, c, :], mean_t[:, g, c, :], ident_bf[:])
-            nc.vector.tensor_copy(out=mean_sb[:, g, :], in_=mean_ps[:].rearrange("b c m -> b (c m)"))
+                nc.tensor.transpose(
+                    mean_ps[:, :, c * quarter : (c + 1) * quarter],
+                    mean_t[:, g, c, :],
+                    sort_k[:].rearrange("m t i -> m (t i)"),
+                )
+            nc.vector.tensor_copy(out=mean_sb[:, g], in_=mean_ps[:])
         bb_grouped = keep.tile([P, BB_PASSES, P, PACK], BF16, name="bb_grouped", align_bytes=64)
         bb_codes = keep.tile([P, BB_PASSES, P], U32, name="bb_codes", align_bytes=64)
         bb_scales = keep.tile([P, BB_PASSES, P], U8, name="bb_scales", align_bytes=64)
         for g in range(BB_PASSES):
             bb_t_ps = psum_main.tile([P, PACK, P], BF16, name="bb_t_ps", tag="main")
             for t in range(PACK):
-                nc.tensor.transpose(bb_t_ps[:, t, :], mean_sb[:, g, t:K_PASS:PACK], ident_bf[:])
+                nc.tensor.transpose(bb_t_ps[:, t, :], mean_sb[:, g, t, :], ident_bf[:])
             nc.vector.tensor_copy(out=bb_grouped[:, g], in_=bb_t_ps[:].rearrange("p t b -> p b t"))
         for g in range(BB_PASSES):
             nc.vector.quantize_mx(

@@ -152,21 +152,24 @@ def tile_gnn_layer_pa_kernel(
             in_=rf_grouped[:].rearrange("p g b t -> p (g b t)"),
         )
 
-        def product(x_codes, x_scales, w_words, w_planes, passes, name):
+        def product(x_codes, x_scales, w_words, w_planes, passes, bank_by_bank, name):
             banks = []
             for c in range(N_TILES):
                 banks.append(psum_main.tile([P, N_TILE], F32, name="%s_%d" % (name, c), tag="main"))
-            for g in range(passes):
-                for c in range(N_TILES):
-                    nc.tensor.matmul_mx(
-                        out=banks[c][:],
-                        lhsT=x_codes[:, g, :].bitcast(FP8X4),
-                        lhsT_scale=x_scales[:, g, :],
-                        rhs=w_words[:, g, 2 * c * N_TILE : 2 * (c + 1) * N_TILE].bitcast(FP4X4),
-                        rhs_scale=w_planes[:, g, c * N_TILE : (c + 1) * N_TILE],
-                        start=(g == 0),
-                        stop=(g == passes - 1),
-                    )
+            if bank_by_bank:
+                order = [(g, c) for c in range(N_TILES) for g in range(passes)]
+            else:
+                order = [(g, c) for g in range(passes) for c in range(N_TILES)]
+            for g, c in order:
+                nc.tensor.matmul_mx(
+                    out=banks[c][:],
+                    lhsT=x_codes[:, g, :].bitcast(FP8X4),
+                    lhsT_scale=x_scales[:, g, :],
+                    rhs=w_words[:, g, 2 * c * N_TILE : 2 * (c + 1) * N_TILE].bitcast(FP4X4),
+                    rhs_scale=w_planes[:, g, c * N_TILE : (c + 1) * N_TILE],
+                    start=(g == 0),
+                    stop=(g == passes - 1),
+                )
             return banks
 
         def add_bias_and_exp(banks, bias, z, w):
@@ -180,7 +183,7 @@ def tile_gnn_layer_pa_kernel(
 
         z_rf = keep.tile([P, DR], F32, name="z_rf")
         w_rf = keep.tile([P, DR], F32, name="w_rf")
-        rf_banks = product(rf_codes, rf_scales, wrf_words, wrf_planes, RF_PASSES, "rf_acc")
+        rf_banks = product(rf_codes, rf_scales, wrf_words, wrf_planes, RF_PASSES, False, "rf_acc")
         add_bias_and_exp(rf_banks, bias_all[:, 0:DR], z_rf, w_rf)
         nc.scalar.activation(out=w_rf[:], in_=w_rf[:], func=ACT.Ln, bias=1.0)
         nc.scalar.activation(out=w_rf[:], in_=w_rf[:], func=ACT.Tanh)
@@ -229,13 +232,16 @@ def tile_gnn_layer_pa_kernel(
 
         z_bb = keep.tile([P, DR], F32, name="z_bb")
         w_bb = keep.tile([P, DR], F32, name="w_bb")
-        bb_banks = product(bb_codes, bb_scales, wbb_words, wbb_planes, BB_PASSES, "bb_acc")
+        bb_banks = product(bb_codes, bb_scales, wbb_words, wbb_planes, BB_PASSES, True, "bb_acc")
         add_bias_and_exp(bb_banks, bias_all[:, DR : 2 * DR], z_bb, w_bb)
         nc.vector.tensor_tensor(out=w_rf[:], in0=w_rf[:], in1=z_rf[:], op=ALU.mult)
         nc.scalar.activation(out=w_bb[:], in_=w_bb[:], func=ACT.Ln, bias=1.0)
-        for c in range(N_TILES):
-            cols = slice(c * N_TILE, (c + 1) * N_TILE)
-            nc.scalar.activation(out=w_bb[:, cols], in_=w_bb[:, cols], func=ACT.Tanh)
-            nc.vector.tensor_tensor(out=w_bb[:, cols], in0=w_bb[:, cols], in1=z_bb[:, cols], op=ALU.mult)
-            nc.vector.tensor_tensor(out=w_bb[:, cols], in0=w_bb[:, cols], in1=w_rf[:, cols], op=ALU.add)
-            nc.sync.dma_start(out=out[:, cols], in_=w_bb[:, cols])
+        for c in range(N_TILES + 1):
+            if c < N_TILES:
+                cols = slice(c * N_TILE, (c + 1) * N_TILE)
+                nc.scalar.activation(out=w_bb[:, cols], in_=w_bb[:, cols], func=ACT.Tanh)
+                nc.vector.tensor_tensor(out=w_bb[:, cols], in0=w_bb[:, cols], in1=z_bb[:, cols], op=ALU.mult)
+            if c > 0:
+                cols = slice((c - 1) * N_TILE, c * N_TILE)
+                nc.vector.tensor_tensor(out=w_bb[:, cols], in0=w_bb[:, cols], in1=w_rf[:, cols], op=ALU.add)
+                nc.sync.dma_start(out=out[:, cols], in_=w_bb[:, cols])

@@ -27,7 +27,6 @@ BB_PASSES = DB // K_PASS
 GROUPS_PER_ROW = 2
 SAMPLES_PER_TILE = P * GROUPS_PER_ROW // GROUPS
 BB_TILES = P // SAMPLES_PER_TILE
-K_CHUNKS = DB // P
 EXP_CAP = 2.0**60
 
 FLOPS = 2 * P * DR * DR + 2 * P * DB * DR
@@ -76,8 +75,6 @@ def tile_gnn_layer_pa_kernel(
         make_identity(nc, ident_f32[:])
         ident_bf = keep.tile([P, P], BF16, name="ident_bf")
         nc.vector.tensor_copy(out=ident_bf[:], in_=ident_f32[:])
-        sort_k = keep.tile([P, PACK, P // PACK], BF16, name="sort_k")
-        nc.vector.tensor_copy(out=sort_k[:], in_=ident_f32[:].rearrange("p (i t) -> p t i", t=PACK))
         group_sum = keep.tile([P, SAMPLES_PER_TILE], F32, name="group_sum")
         nc.vector.tensor_reduce(
             out=group_sum[:],
@@ -192,37 +189,21 @@ def tile_gnn_layer_pa_kernel(
         for g in range(BB_PASSES):
             mean_t_ps.append(psum_side.tile([P, PACK, P], F32, name="mean_t_ps_%d" % g, tag="side"))
         for j in range(BB_TILES):
-            for c in range(K_CHUNKS):
-                for i in range(GROUPS_PER_ROW):
-                    nc.tensor.matmul(
-                        out=mean_t_ps[c // PACK][:, c % PACK, j * SAMPLES_PER_TILE : (j + 1) * SAMPLES_PER_TILE],
-                        lhsT=bb_sb[:, j, i, c * P : (c + 1) * P],
-                        rhs=group_mean[:],
-                        start=(i == 0),
-                        stop=(i == GROUPS_PER_ROW - 1),
-                    )
-        mean_t = keep.tile([P, BB_PASSES, PACK, P], BF16, name="mean_t")
-        for g in range(BB_PASSES):
-            nc.vector.tensor_copy(out=mean_t[:, g], in_=mean_t_ps[g][:])
-        quarter = P // PACK
-        mean_sb = keep.tile([P, BB_PASSES, PACK, P], BF16, name="mean_sb")
-        for g in range(BB_PASSES):
-            mean_ps = psum_main.tile([P, PACK, P], BF16, name="mean_ps", tag="main")
-            for c in range(PACK):
-                nc.tensor.transpose(
-                    mean_ps[:, :, c * quarter : (c + 1) * quarter],
-                    mean_t[:, g, c, :],
-                    sort_k[:].rearrange("m t i -> m (t i)"),
-                )
-            nc.vector.tensor_copy(out=mean_sb[:, g], in_=mean_ps[:])
+            for g in range(BB_PASSES):
+                for t in range(PACK):
+                    for i in range(GROUPS_PER_ROW):
+                        nc.tensor.matmul(
+                            out=mean_t_ps[g][:, t, j * SAMPLES_PER_TILE : (j + 1) * SAMPLES_PER_TILE],
+                            lhsT=bb_sb[:, j, i, g * K_PASS + t : (g + 1) * K_PASS : PACK],
+                            rhs=group_mean[:],
+                            start=(i == 0),
+                            stop=(i == GROUPS_PER_ROW - 1),
+                        )
         bb_grouped = keep.tile([P, BB_PASSES, P, PACK], BF16, name="bb_grouped", align_bytes=64)
         bb_codes = keep.tile([P, BB_PASSES, P], U32, name="bb_codes", align_bytes=64)
         bb_scales = keep.tile([P, BB_PASSES, P], U8, name="bb_scales", align_bytes=64)
         for g in range(BB_PASSES):
-            bb_t_ps = psum_main.tile([P, PACK, P], BF16, name="bb_t_ps", tag="main")
-            for t in range(PACK):
-                nc.tensor.transpose(bb_t_ps[:, t, :], mean_sb[:, g, t, :], ident_bf[:])
-            nc.vector.tensor_copy(out=bb_grouped[:, g], in_=bb_t_ps[:].rearrange("p t b -> p b t"))
+            nc.vector.tensor_copy(out=bb_grouped[:, g], in_=mean_t_ps[g][:].rearrange("p t b -> p b t"))
         for g in range(BB_PASSES):
             nc.vector.quantize_mx(
                 out=bb_codes[:, g, :].bitcast(FP8X4),

@@ -27,6 +27,7 @@ BB_PASSES = DB // K_PASS
 GROUPS_PER_ROW = 2
 SAMPLES_PER_TILE = P * GROUPS_PER_ROW // GROUPS
 BB_TILES = P // SAMPLES_PER_TILE
+
 EXP_CAP = 2.0**60
 
 FLOPS = 2 * P * DR * DR + 2 * P * DB * DR
@@ -58,6 +59,7 @@ def tile_gnn_layer_pa_kernel(
         keep = ctx.enter_context(tc.tile_pool(name="keep", bufs=1))
         psum_main = ctx.enter_context(tc.psum_pool(name="psum_main", bufs=4))
         psum_side = ctx.enter_context(tc.psum_pool(name="psum_side", bufs=2))
+        psum_bias = ctx.enter_context(tc.psum_pool(name="psum_bias", bufs=2))
         ctx.enter_context(tc.manual_schedule())
 
         rf_sb = keep.tile([P, DR], BF16, name="rf_sb")
@@ -86,8 +88,8 @@ def tile_gnn_layer_pa_kernel(
         nc.vector.tensor_scalar_mul(out=group_mean[:], in0=group_sum[:], scalar1=1.0 / GROUPS)
 
         bias_chunks = DR // P
-        nc.sync.dma_start(out=bias_rows[0:bias_chunks, :], in_=b_rfrf.rearrange("(r c) -> r c", c=P))
-        nc.sync.dma_start(
+        nc.scalar.dma_start(out=bias_rows[0:bias_chunks, :], in_=b_rfrf.rearrange("(r c) -> r c", c=P))
+        nc.scalar.dma_start(
             out=bias_rows[bias_chunks : 2 * bias_chunks, :], in_=b_bbrf.rearrange("(r c) -> r c", c=P)
         )
         nc.sync.dma_start(out=rf_sb[:], in_=RF_feature)
@@ -102,25 +104,6 @@ def tile_gnn_layer_pa_kernel(
         load_scale_planes(nc, wbb_planes, W_bbrf_scales)
         for g in range(BB_PASSES):
             nc.sync.dma_start(out=wbb_words[:, g, :].bitcast(I32), in_=W_bbrf_words[g].bitcast(I32))
-
-        bias_cols_ps = psum_side.tile([P, P], BF16, name="bias_cols_ps", tag="side")
-        nc.tensor.transpose(bias_cols_ps[:], bias_rows[:], ident_bf[:])
-        bias_cols = keep.tile([P, 2 * bias_chunks], BF16, name="bias_cols")
-        nc.vector.tensor_copy(out=bias_cols[:], in_=bias_cols_ps[:, 0 : 2 * bias_chunks])
-        bias_all = keep.tile([P, 2 * DR], BF16, name="bias_all")
-        chunks_per_bank = 8
-        for bank in range(2 * bias_chunks // chunks_per_bank):
-            spread_ps = psum_main.tile([P, chunks_per_bank * P], BF16, name="spread_ps", tag="main")
-            for i in range(chunks_per_bank):
-                j = bank * chunks_per_bank + i
-                nc.tensor.transpose(
-                    spread_ps[:, i * P : (i + 1) * P], bias_cols[:, j : j + 1].to_broadcast([P, P]), ident_bf[:]
-                )
-            cols = slice(bank * chunks_per_bank * P, (bank + 1) * chunks_per_bank * P)
-            if bank % 2 == 0:
-                nc.scalar.copy(out=bias_all[:, cols], in_=spread_ps[:])
-            else:
-                nc.vector.tensor_copy(out=bias_all[:, cols], in_=spread_ps[:])
 
         rf_words = rf_sb[:].bitcast(F32)
         rf_grouped = keep.tile([P, RF_PASSES, P, PACK], BF16, name="rf_grouped", align_bytes=64)
@@ -141,6 +124,27 @@ def tile_gnn_layer_pa_kernel(
                 nc.vector.tensor_copy(out=dst, in_=src)
             else:
                 nc.scalar.copy(out=dst, in_=src)
+
+        bias_cols_ps = psum_side.tile([P, P], BF16, name="bias_cols_ps", tag="side")
+        nc.tensor.transpose(bias_cols_ps[:], bias_rows[:], ident_bf[:])
+        bias_cols = keep.tile([P, 2 * bias_chunks], BF16, name="bias_cols")
+        nc.vector.tensor_copy(out=bias_cols[:], in_=bias_cols_ps[:, 0 : 2 * bias_chunks])
+        bias_all = keep.tile([P, 2 * DR], BF16, name="bias_all")
+        chunks_per_bank = 8
+
+        def spread_bias(bank, pool, tag, on_scalar):
+            spread_ps = pool.tile([P, chunks_per_bank * P], BF16, name="spread_ps", tag=tag)
+            for i in range(chunks_per_bank):
+                j = bank * chunks_per_bank + i
+                nc.tensor.transpose(
+                    spread_ps[:, i * P : (i + 1) * P], bias_cols[:, j : j + 1].to_broadcast([P, P]), ident_bf[:]
+                )
+            cols = slice(bank * chunks_per_bank * P, (bank + 1) * chunks_per_bank * P)
+            if on_scalar:
+                nc.scalar.copy(out=bias_all[:, cols], in_=spread_ps[:])
+            else:
+                nc.vector.tensor_copy(out=bias_all[:, cols], in_=spread_ps[:])
+
         rf_codes = keep.tile([P, RF_PASSES, P], U32, name="rf_codes", align_bytes=64)
         rf_scales = keep.tile([P, RF_PASSES, P], U8, name="rf_scales", align_bytes=64)
         nc.vector.quantize_mx(
@@ -148,6 +152,8 @@ def tile_gnn_layer_pa_kernel(
             scales=rf_scales[:].rearrange("p g b -> p (g b)"),
             in_=rf_grouped[:].rearrange("p g b t -> p (g b t)"),
         )
+        spread_bias(0, psum_main, "main", True)
+        spread_bias(1, psum_main, "main", False)
 
         def product(x_codes, x_scales, w_words, w_planes, passes, bank_by_bank, name):
             banks = []
@@ -169,21 +175,55 @@ def tile_gnn_layer_pa_kernel(
                 )
             return banks
 
-        def add_bias_and_exp(banks, bias, z, w):
-            for c in range(N_TILES):
-                cols = slice(c * N_TILE, (c + 1) * N_TILE)
-                nc.vector.tensor_tensor(out=z[:, cols], in0=banks[c][:], in1=bias[:, cols], op=ALU.add)
-                nc.scalar.activation(out=w[:, cols], in_=z[:, cols], func=ACT.Exp)
-            for c in range(N_TILES):
-                cols = slice(c * N_TILE, (c + 1) * N_TILE)
-                nc.vector.tensor_scalar_min(out=w[:, cols], in0=w[:, cols], scalar1=EXP_CAP)
+        def tile_cols(c):
+            return slice(c * N_TILE, (c + 1) * N_TILE)
+
+        def add_bias_exp_and_n(banks, bias, z, w):
+            for c in range(N_TILES + 1):
+                if c < N_TILES:
+                    cols = tile_cols(c)
+                    nc.vector.tensor_tensor(out=z[:, cols], in0=banks[c][:], in1=bias[:, cols], op=ALU.add)
+                    nc.scalar.activation(out=w[:, cols], in_=z[:, cols], func=ACT.Exp)
+                if c > 0:
+                    cols = tile_cols(c - 1)
+                    nc.vector.scalar_tensor_tensor(
+                        out=w[:, cols], in0=w[:, cols], scalar=2.0, in1=w[:, cols], op0=ALU.add, op1=ALU.mult
+                    )
+
+        def finish_term(w, z, rest, store):
+            for c in range(N_TILES + 1):
+                if c < N_TILES:
+                    cols = tile_cols(c)
+                    nc.scalar.activation(out=w[:, cols], in_=w[:, cols], func=ACT.Abs_reciprocal_sqrt, bias=2.0)
+                if c > 0:
+                    cols = tile_cols(c - 1)
+                    nc.scalar.activation(out=w[:, cols], in_=w[:, cols], func=ACT.Square)
+            for c in range(N_TILES + 1):
+                if c < N_TILES:
+                    cols = tile_cols(c)
+                    nc.vector.tensor_tensor(out=w[:, cols], in0=w[:, cols], in1=z[:, cols], op=ALU.mult)
+                if c > 0:
+                    cols = tile_cols(c - 1)
+                    nc.vector.scalar_tensor_tensor(
+                        out=w[:, cols], in0=w[:, cols], scalar=-2.0, in1=rest[:, cols], op0=ALU.mult, op1=ALU.add
+                    )
+                    if store:
+                        nc.sync.dma_start(out=out[:, cols], in_=w[:, cols])
 
         z_rf = keep.tile([P, DR], F32, name="z_rf")
         w_rf = keep.tile([P, DR], F32, name="w_rf")
         rf_banks = product(rf_codes, rf_scales, wrf_words, wrf_planes, RF_PASSES, False, "rf_acc")
-        add_bias_and_exp(rf_banks, bias_all[:, 0:DR], z_rf, w_rf)
+        for c in range(N_TILES):
+            cols = tile_cols(c)
+            nc.vector.tensor_tensor(out=z_rf[:, cols], in0=rf_banks[c][:], in1=bias_all[:, cols], op=ALU.add)
+            nc.scalar.activation(out=w_rf[:, cols], in_=z_rf[:, cols], func=ACT.Exp)
+        for c in range(N_TILES):
+            cols = tile_cols(c)
+            nc.vector.tensor_scalar_min(out=w_rf[:, cols], in0=w_rf[:, cols], scalar1=EXP_CAP)
         nc.scalar.activation(out=w_rf[:], in_=w_rf[:], func=ACT.Ln, bias=1.0)
-        nc.scalar.activation(out=w_rf[:], in_=w_rf[:], func=ACT.Tanh)
+        for c in range(N_TILES):
+            cols = tile_cols(c)
+            nc.scalar.activation(out=w_rf[:, cols], in_=w_rf[:, cols], func=ACT.Tanh)
 
         mean_t_ps = []
         for g in range(BB_PASSES):
@@ -199,6 +239,8 @@ def tile_gnn_layer_pa_kernel(
                             start=(i == 0),
                             stop=(i == GROUPS_PER_ROW - 1),
                         )
+        spread_bias(2, psum_bias, "bias", True)
+        spread_bias(3, psum_bias, "bias", True)
         bb_grouped = keep.tile([P, BB_PASSES, P, PACK], BF16, name="bb_grouped", align_bytes=64)
         bb_codes = keep.tile([P, BB_PASSES, P], U32, name="bb_codes", align_bytes=64)
         bb_scales = keep.tile([P, BB_PASSES, P], U8, name="bb_scales", align_bytes=64)
@@ -211,18 +253,15 @@ def tile_gnn_layer_pa_kernel(
                 in_=bb_grouped[:, g].rearrange("p b t -> p (b t)"),
             )
 
+        for c in range(N_TILES):
+            cols = tile_cols(c)
+            nc.vector.tensor_tensor(out=w_rf[:, cols], in0=w_rf[:, cols], in1=z_rf[:, cols], op=ALU.mult)
+
         z_bb = keep.tile([P, DR], F32, name="z_bb")
         w_bb = keep.tile([P, DR], F32, name="w_bb")
         bb_banks = product(bb_codes, bb_scales, wbb_words, wbb_planes, BB_PASSES, True, "bb_acc")
-        add_bias_and_exp(bb_banks, bias_all[:, DR : 2 * DR], z_bb, w_bb)
-        nc.vector.tensor_tensor(out=w_rf[:], in0=w_rf[:], in1=z_rf[:], op=ALU.mult)
-        nc.scalar.activation(out=w_bb[:], in_=w_bb[:], func=ACT.Ln, bias=1.0)
-        for c in range(N_TILES + 1):
-            if c < N_TILES:
-                cols = slice(c * N_TILE, (c + 1) * N_TILE)
-                nc.scalar.activation(out=w_bb[:, cols], in_=w_bb[:, cols], func=ACT.Tanh)
-                nc.vector.tensor_tensor(out=w_bb[:, cols], in0=w_bb[:, cols], in1=z_bb[:, cols], op=ALU.mult)
-            if c > 0:
-                cols = slice((c - 1) * N_TILE, c * N_TILE)
-                nc.vector.tensor_tensor(out=w_bb[:, cols], in0=w_bb[:, cols], in1=w_rf[:, cols], op=ALU.add)
-                nc.sync.dma_start(out=out[:, cols], in_=w_bb[:, cols])
+        add_bias_exp_and_n(bb_banks, bias_all[:, DR : 2 * DR], z_bb, w_bb)
+        for c in range(N_TILES):
+            cols = tile_cols(c)
+            nc.vector.tensor_tensor(out=w_rf[:, cols], in0=w_rf[:, cols], in1=z_bb[:, cols], op=ALU.add)
+        finish_term(w_bb, z_bb, w_rf, True)

@@ -58,8 +58,7 @@ def tile_gnn_layer_pa_kernel(
     with ExitStack() as ctx:
         keep = ctx.enter_context(tc.tile_pool(name="keep", bufs=1))
         psum_main = ctx.enter_context(tc.psum_pool(name="psum_main", bufs=4))
-        psum_side = ctx.enter_context(tc.psum_pool(name="psum_side", bufs=2))
-        psum_bias = ctx.enter_context(tc.psum_pool(name="psum_bias", bufs=2))
+        psum_side = ctx.enter_context(tc.psum_pool(name="psum_side", bufs=4))
         ctx.enter_context(tc.manual_schedule())
 
         rf_sb = keep.tile([P, DR], BF16, name="rf_sb")
@@ -89,9 +88,6 @@ def tile_gnn_layer_pa_kernel(
 
         bias_chunks = DR // P
         nc.scalar.dma_start(out=bias_rows[0:bias_chunks, :], in_=b_rfrf.rearrange("(r c) -> r c", c=P))
-        nc.scalar.dma_start(
-            out=bias_rows[bias_chunks : 2 * bias_chunks, :], in_=b_bbrf.rearrange("(r c) -> r c", c=P)
-        )
         nc.sync.dma_start(out=rf_sb[:], in_=RF_feature)
         load_scale_planes(nc, wrf_planes, W_rfrf_scales)
         for g in range(RF_PASSES):
@@ -102,8 +98,12 @@ def tile_gnn_layer_pa_kernel(
                 out=bb_sb[:, j].rearrange("p i k -> p (i k)"), in_=bb_rows[j * P : (j + 1) * P, :]
             )
         load_scale_planes(nc, wbb_planes, W_bbrf_scales)
-        for g in range(BB_PASSES):
-            nc.sync.dma_start(out=wbb_words[:, g, :].bitcast(I32), in_=W_bbrf_words[g].bitcast(I32))
+        for c in range(N_TILES):
+            byte_cols = slice(2 * c * N_TILE, 2 * (c + 1) * N_TILE)
+            nc.sync.dma_start(
+                out=wbb_words[:, :, byte_cols].bitcast(I32),
+                in_=W_bbrf_words[:, :, byte_cols].bitcast(I32).rearrange("g p n -> p g n"),
+            )
 
         rf_words = rf_sb[:].bitcast(F32)
         rf_grouped = keep.tile([P, RF_PASSES, P, PACK], BF16, name="rf_grouped", align_bytes=64)
@@ -127,8 +127,8 @@ def tile_gnn_layer_pa_kernel(
 
         bias_cols_ps = psum_side.tile([P, P], BF16, name="bias_cols_ps", tag="side")
         nc.tensor.transpose(bias_cols_ps[:], bias_rows[:], ident_bf[:])
-        bias_cols = keep.tile([P, 2 * bias_chunks], BF16, name="bias_cols")
-        nc.vector.tensor_copy(out=bias_cols[:], in_=bias_cols_ps[:, 0 : 2 * bias_chunks])
+        bias_cols = keep.tile([P, bias_chunks], BF16, name="bias_cols")
+        nc.vector.tensor_copy(out=bias_cols[:], in_=bias_cols_ps[:, 0:bias_chunks])
         bias_all = keep.tile([P, 2 * DR], BF16, name="bias_all")
         chunks_per_bank = 8
 
@@ -154,6 +154,11 @@ def tile_gnn_layer_pa_kernel(
         )
         spread_bias(0, psum_main, "main", True)
         spread_bias(1, psum_main, "main", False)
+        bbb_row = keep.tile([P, DR], BF16, name="bbb_row")
+        nc.vector.memset(bbb_row[:].bitcast(I32), 0)
+        ones = keep.tile([P, P], BF16, name="ones")
+        nc.vector.memset(ones[:], 1.0)
+        nc.scalar.dma_start(out=bbb_row[0:1, :], in_=b_bbrf.rearrange("(r c) -> r c", r=1))
 
         def product(x_codes, x_scales, w_words, w_planes, passes, bank_by_bank, name):
             banks = []
@@ -225,33 +230,50 @@ def tile_gnn_layer_pa_kernel(
             cols = tile_cols(c)
             nc.scalar.activation(out=w_rf[:, cols], in_=w_rf[:, cols], func=ACT.Tanh)
 
-        mean_t_ps = []
-        for g in range(BB_PASSES):
-            mean_t_ps.append(psum_side.tile([P, PACK, P], F32, name="mean_t_ps_%d" % g, tag="side"))
-        for j in range(BB_TILES):
-            for g in range(BB_PASSES):
-                for t in range(PACK):
-                    for i in range(GROUPS_PER_ROW):
-                        nc.tensor.matmul(
-                            out=mean_t_ps[g][:, t, j * SAMPLES_PER_TILE : (j + 1) * SAMPLES_PER_TILE],
-                            lhsT=bb_sb[:, j, i, g * K_PASS + t : (g + 1) * K_PASS : PACK],
-                            rhs=group_mean[:],
-                            start=(i == 0),
-                            stop=(i == GROUPS_PER_ROW - 1),
-                        )
-        spread_bias(2, psum_bias, "bias", True)
-        spread_bias(3, psum_bias, "bias", True)
         bb_grouped = keep.tile([P, BB_PASSES, P, PACK], BF16, name="bb_grouped", align_bytes=64)
         bb_codes = keep.tile([P, BB_PASSES, P], U32, name="bb_codes", align_bytes=64)
         bb_scales = keep.tile([P, BB_PASSES, P], U8, name="bb_scales", align_bytes=64)
-        for g in range(BB_PASSES):
-            nc.vector.tensor_copy(out=bb_grouped[:, g], in_=mean_t_ps[g][:].rearrange("p t b -> p b t"))
-        for g in range(BB_PASSES):
-            nc.vector.quantize_mx(
-                out=bb_codes[:, g, :].bitcast(FP8X4),
-                scales=bb_scales[:, g, :],
-                in_=bb_grouped[:, g].rearrange("p b t -> p (b t)"),
-            )
+        tiles_per_half = BB_TILES // 2
+        half_samples = P // 2
+        for half in range(2):
+            mean_t_ps = []
+            for g in range(BB_PASSES):
+                mean_t_ps.append(psum_side.tile([P, PACK, half_samples], F32, name="mean_t_ps_%d" % g, tag="side"))
+            for j_in in range(tiles_per_half):
+                j = half * tiles_per_half + j_in
+                for g in range(BB_PASSES):
+                    for t in range(PACK):
+                        for i in range(GROUPS_PER_ROW):
+                            nc.tensor.matmul(
+                                out=mean_t_ps[g][:, t, j_in * SAMPLES_PER_TILE : (j_in + 1) * SAMPLES_PER_TILE],
+                                lhsT=bb_sb[:, j, i, g * K_PASS + t : (g + 1) * K_PASS : PACK],
+                                rhs=group_mean[:],
+                                start=(i == 0),
+                                stop=(i == GROUPS_PER_ROW - 1),
+                            )
+            samples = slice(half * half_samples, (half + 1) * half_samples)
+            for g in range(BB_PASSES):
+                nc.vector.tensor_copy(
+                    out=bb_grouped[:, g, samples, :], in_=mean_t_ps[g][:].rearrange("p t b -> p b t")
+                )
+            for g in range(BB_PASSES):
+                nc.vector.quantize_mx(
+                    out=bb_codes[:, g, samples].bitcast(FP8X4),
+                    scales=bb_scales[:, g, samples],
+                    in_=bb_grouped[:, g, samples, :].rearrange("p b t -> p (b t)"),
+                )
+        for bank in range(2):
+            bbb_ps = psum_side.tile([P, 2 * N_TILE], BF16, name="bbb_ps", tag="side")
+            for i in range(2):
+                c = 2 * bank + i
+                nc.tensor.matmul(
+                    out=bbb_ps[:, i * N_TILE : (i + 1) * N_TILE],
+                    lhsT=ones[:],
+                    rhs=bbb_row[:, c * N_TILE : (c + 1) * N_TILE],
+                    start=True,
+                    stop=True,
+                )
+            nc.scalar.copy(out=bias_all[:, DR + 2 * bank * N_TILE : DR + 2 * (bank + 1) * N_TILE], in_=bbb_ps[:])
 
         for c in range(N_TILES):
             cols = tile_cols(c)

@@ -195,25 +195,27 @@ def tile_gnn_layer_pa_kernel(
                         out=w[:, cols], in0=w[:, cols], scalar=2.0, in1=w[:, cols], op0=ALU.add, op1=ALU.mult
                     )
 
-        def finish_term(w, z, rest, store):
-            for c in range(N_TILES + 1):
-                if c < N_TILES:
-                    cols = tile_cols(c)
-                    nc.scalar.activation(out=w[:, cols], in_=w[:, cols], func=ACT.Abs_reciprocal_sqrt, bias=2.0)
-                if c > 0:
-                    cols = tile_cols(c - 1)
-                    nc.scalar.activation(out=w[:, cols], in_=w[:, cols], func=ACT.Square)
-            for c in range(N_TILES + 1):
-                if c < N_TILES:
-                    cols = tile_cols(c)
-                    nc.vector.tensor_tensor(out=w[:, cols], in0=w[:, cols], in1=z[:, cols], op=ALU.mult)
-                if c > 0:
-                    cols = tile_cols(c - 1)
-                    nc.vector.scalar_tensor_tensor(
-                        out=w[:, cols], in0=w[:, cols], scalar=-2.0, in1=rest[:, cols], op0=ALU.mult, op1=ALU.add
+        def finish_term(w, z, rest):
+            pieces = [tile_cols(c) for c in range(N_TILES - 1)]
+            pieces.append(slice(DR - N_TILE, DR - N_TILE // 2))
+            pieces.append(slice(DR - N_TILE // 2, DR))
+            for i in range(len(pieces) + 1):
+                if i < len(pieces):
+                    cols = pieces[i]
+                    nc.scalar.activation(
+                        out=w[:, cols], in_=w[:, cols], func=ACT.Abs_reciprocal_sqrt, scale=0.5, bias=1.0
                     )
-                    if store:
-                        nc.sync.dma_start(out=out[:, cols], in_=w[:, cols])
+                if i > 0:
+                    cols = pieces[i - 1]
+                    nc.scalar.activation(out=w[:, cols], in_=w[:, cols], func=ACT.Square)
+            for i in range(len(pieces) + 1):
+                if i < len(pieces):
+                    cols = pieces[i]
+                    nc.vector.tensor_tensor(out=w[:, cols], in0=w[:, cols], in1=z[:, cols], op=ALU.mult)
+                if i > 0:
+                    cols = pieces[i - 1]
+                    nc.vector.tensor_tensor(out=w[:, cols], in0=rest[:, cols], in1=w[:, cols], op=ALU.subtract)
+                    nc.sync.dma_start(out=out[:, cols], in_=w[:, cols])
 
         z_rf = keep.tile([P, DR], F32, name="z_rf")
         w_rf = keep.tile([P, DR], F32, name="w_rf")
@@ -286,4 +288,4 @@ def tile_gnn_layer_pa_kernel(
         for c in range(N_TILES):
             cols = tile_cols(c)
             nc.vector.tensor_tensor(out=w_rf[:, cols], in0=w_rf[:, cols], in1=z_bb[:, cols], op=ALU.add)
-        finish_term(w_bb, z_bb, w_rf, True)
+        finish_term(w_bb, z_bb, w_rf)

@@ -237,12 +237,28 @@ def tile_gnn_layer_pa_kernel(
         bb_scales = keep.tile([P, BB_PASSES, P], U8, name="bb_scales", align_bytes=64)
         tiles_per_half = BB_TILES // 2
         half_samples = P // 2
+
+        def spread_b_bbrf(bank):
+            bbb_ps = psum_side.tile([P, 2 * N_TILE], BF16, name="bbb_ps", tag="side")
+            for i in range(2):
+                c = 2 * bank + i
+                nc.tensor.matmul(
+                    out=bbb_ps[:, i * N_TILE : (i + 1) * N_TILE],
+                    lhsT=ones[:],
+                    rhs=bbb_row[:, c * N_TILE : (c + 1) * N_TILE],
+                    start=True,
+                    stop=True,
+                )
+            nc.scalar.copy(out=bias_all[:, DR + 2 * bank * N_TILE : DR + 2 * (bank + 1) * N_TILE], in_=bbb_ps[:])
+
         for half in range(2):
             mean_t_ps = []
             for g in range(BB_PASSES):
                 mean_t_ps.append(psum_side.tile([P, PACK, half_samples], F32, name="mean_t_ps_%d" % g, tag="side"))
             for j_in in range(tiles_per_half):
                 j = half * tiles_per_half + j_in
+                if j == BB_TILES - 1:
+                    spread_b_bbrf(0)
                 for g in range(BB_PASSES):
                     for t in range(PACK):
                         for i in range(GROUPS_PER_ROW):
@@ -264,18 +280,7 @@ def tile_gnn_layer_pa_kernel(
                     scales=bb_scales[:, g, samples],
                     in_=bb_grouped[:, g, samples, :].rearrange("p b t -> p (b t)"),
                 )
-        for bank in range(2):
-            bbb_ps = psum_side.tile([P, 2 * N_TILE], BF16, name="bbb_ps", tag="side")
-            for i in range(2):
-                c = 2 * bank + i
-                nc.tensor.matmul(
-                    out=bbb_ps[:, i * N_TILE : (i + 1) * N_TILE],
-                    lhsT=ones[:],
-                    rhs=bbb_row[:, c * N_TILE : (c + 1) * N_TILE],
-                    start=True,
-                    stop=True,
-                )
-            nc.scalar.copy(out=bias_all[:, DR + 2 * bank * N_TILE : DR + 2 * (bank + 1) * N_TILE], in_=bbb_ps[:])
+        spread_b_bbrf(1)
 
         for c in range(N_TILES):
             cols = tile_cols(c)

@@ -33,12 +33,11 @@ EXP_CAP = 2.0**60
 FLOPS = 2 * P * DR * DR + 2 * P * DB * DR
 
 
-def load_scale_planes(nc, planes, scales):
-    words = scales.bitcast(I32)
+def load_scale_planes(nc, planes, scales, cols):
     for r in range(4):
         nc.sync.dma_start(
-            out=planes[r:P:32, :, :].bitcast(I32),
-            in_=words[:, r:16:4, :].rearrange("g q n -> q g n"),
+            out=planes[r:P:32, :, cols].bitcast(I32),
+            in_=scales[:, r:16:4, cols].bitcast(I32).rearrange("g q n -> q g n"),
         )
 
 
@@ -89,7 +88,7 @@ def tile_gnn_layer_pa_kernel(
         bias_chunks = DR // P
         nc.scalar.dma_start(out=bias_rows[0:bias_chunks, :], in_=b_rfrf.rearrange("(r c) -> r c", c=P))
         nc.sync.dma_start(out=rf_sb[:], in_=RF_feature)
-        load_scale_planes(nc, wrf_planes, W_rfrf_scales)
+        load_scale_planes(nc, wrf_planes, W_rfrf_scales, slice(0, DR))
         for g in range(RF_PASSES):
             nc.sync.dma_start(out=wrf_words[:, g, :].bitcast(I32), in_=W_rfrf_words[g].bitcast(I32))
         bb_rows = BB_feature.rearrange("b (h i) k -> (b h) (i k)", i=GROUPS_PER_ROW)
@@ -97,8 +96,9 @@ def tile_gnn_layer_pa_kernel(
             nc.sync.dma_start(
                 out=bb_sb[:, j].rearrange("p i k -> p (i k)"), in_=bb_rows[j * P : (j + 1) * P, :]
             )
-        load_scale_planes(nc, wbb_planes, W_bbrf_scales)
         for c in range(N_TILES):
+            if c % 2 == 0:
+                load_scale_planes(nc, wbb_planes, W_bbrf_scales, slice(c * N_TILE, (c + 2) * N_TILE))
             byte_cols = slice(2 * c * N_TILE, 2 * (c + 1) * N_TILE)
             nc.sync.dma_start(
                 out=wbb_words[:, :, byte_cols].bitcast(I32),

from contextlib import ExitStack

import concourse.mybir as mybir
from concourse.masks import make_identity

F32 = mybir.dt.float32
BF16 = mybir.dt.bfloat16
I32 = mybir.dt.int32
U32 = mybir.dt.uint32
U8 = mybir.dt.uint8
FP8X4 = mybir.dt.float8_e4m3fn_x4
FP4X4 = mybir.dt.float4_e2m1fn_x4
ACT = mybir.ActivationFunctionType
ALU = mybir.AluOpType
AXIS = mybir.AxisListType

P = 128
PACK = 4
K_PASS = P * PACK
GROUPS = 16
DB = 1024
DR = 2048
N_TILE = 512
N_TILES = DR // N_TILE
RF_PASSES = DR // K_PASS
BB_PASSES = DB // K_PASS
GROUPS_PER_ROW = 2
SAMPLES_PER_TILE = P * GROUPS_PER_ROW // GROUPS
BB_TILES = P // SAMPLES_PER_TILE

EXP_CAP = 2.0**60

FLOPS = 2 * P * DR * DR + 2 * P * DB * DR


def load_scale_planes(nc, planes, scales, cols):
    for r in range(4):
        nc.sync.dma_start(
            out=planes[r:P:32, :, cols].bitcast(I32),
            in_=scales[:, r:16:4, cols].bitcast(I32).rearrange("g q n -> q g n"),
        )


def tile_gnn_layer_pa_kernel(
    tc,
    BB_feature,
    RF_feature,
    W_rfrf_words,
    W_rfrf_scales,
    b_rfrf,
    W_bbrf_words,
    W_bbrf_scales,
    b_bbrf,
    out,
):
    nc = tc.nc
    with ExitStack() as ctx:
        keep = ctx.enter_context(tc.tile_pool(name="keep", bufs=1))
        psum_main = ctx.enter_context(tc.psum_pool(name="psum_main", bufs=4))
        psum_side = ctx.enter_context(tc.psum_pool(name="psum_side", bufs=4))
        ctx.enter_context(tc.manual_schedule())

        rf_sb = keep.tile([P, DR], BF16, name="rf_sb")
        bb_sb = keep.tile([P, BB_TILES, GROUPS_PER_ROW, DB], BF16, name="bb_sb")
        wrf_words = keep.tile([P, RF_PASSES, 2 * DR], U8, name="wrf_words", align_bytes=64)
        wbb_words = keep.tile([P, BB_PASSES, 2 * DR], U8, name="wbb_words", align_bytes=64)
        wrf_planes = keep.tile([P, RF_PASSES, DR], U8, name="wrf_planes", align_bytes=64)
        wbb_planes = keep.tile([P, BB_PASSES, DR], U8, name="wbb_planes", align_bytes=64)
        bias_rows = keep.tile([P, P], BF16, name="bias_rows")

        nc.vector.memset(bias_rows[:], 0.0)
        nc.vector.memset(wrf_planes[:].rearrange("p g n -> p (g n)").bitcast(I32), 0)
        nc.vector.memset(wbb_planes[:].rearrange("p g n -> p (g n)").bitcast(I32), 0)
        ident_f32 = keep.tile([P, P], F32, name="ident_f32")
        make_identity(nc, ident_f32[:])
        ident_bf = keep.tile([P, P], BF16, name="ident_bf")
        nc.vector.tensor_copy(out=ident_bf[:], in_=ident_f32[:])
        group_sum = keep.tile([P, SAMPLES_PER_TILE], F32, name="group_sum")
        nc.vector.tensor_reduce(
            out=group_sum[:],
            in_=ident_f32[:].rearrange("p (i r) -> p i r", i=SAMPLES_PER_TILE),
            axis=AXIS.X,
            op=ALU.add,
        )
        group_mean = keep.tile([P, SAMPLES_PER_TILE], BF16, name="group_mean")
        nc.vector.tensor_scalar_mul(out=group_mean[:], in0=group_sum[:], scalar1=1.0 / GROUPS)

        bias_chunks = DR // P
        nc.scalar.dma_start(out=bias_rows[0:bias_chunks, :], in_=b_rfrf.rearrange("(r c) -> r c", c=P))
        nc.sync.dma_start(out=rf_sb[:], in_=RF_feature)
        load_scale_planes(nc, wrf_planes, W_rfrf_scales, slice(0, DR))
        for g in range(RF_PASSES):
            nc.sync.dma_start(out=wrf_words[:, g, :].bitcast(I32), in_=W_rfrf_words[g].bitcast(I32))
        bb_rows = BB_feature.rearrange("b (h i) k -> (b h) (i k)", i=GROUPS_PER_ROW)
        for j in range(BB_TILES):
            nc.sync.dma_start(
                out=bb_sb[:, j].rearrange("p i k -> p (i k)"), in_=bb_rows[j * P : (j + 1) * P, :]
            )
        for c in range(N_TILES):
            if c % 2 == 0:
                load_scale_planes(nc, wbb_planes, W_bbrf_scales, slice(c * N_TILE, (c + 2) * N_TILE))
            byte_cols = slice(2 * c * N_TILE, 2 * (c + 1) * N_TILE)
            nc.sync.dma_start(
                out=wbb_words[:, :, byte_cols].bitcast(I32),
                in_=W_bbrf_words[:, :, byte_cols].bitcast(I32).rearrange("g p n -> p g n"),
            )

        rf_words = rf_sb[:].bitcast(F32)
        rf_grouped = keep.tile([P, RF_PASSES, P, PACK], BF16, name="rf_grouped", align_bytes=64)
        rf_grouped_words = rf_grouped[:].bitcast(F32)
        for half in range(2):
            rf_t_ps = psum_side.tile([P, 2, 2, P], F32, name="rf_t_ps", tag="side")
            for g_in in range(2):
                g = 2 * half + g_in
                for u in range(2):
                    nc.tensor.transpose(
                        rf_t_ps[:, g_in, u, :],
                        rf_words[:, g * K_PASS // 2 + u : (g + 1) * K_PASS // 2 : 2],
                        ident_f32[:],
                    )
            dst = rf_grouped_words[:, 2 * half : 2 * half + 2, :, :]
            src = rf_t_ps[:].rearrange("p g u b -> p g b u")
            if half == 0:
                nc.vector.tensor_copy(out=dst, in_=src)
            else:
                nc.scalar.copy(out=dst, in_=src)

        bias_cols_ps = psum_side.tile([P, P], BF16, name="bias_cols_ps", tag="side")
        nc.tensor.transpose(bias_cols_ps[:], bias_rows[:], ident_bf[:])
        bias_cols = keep.tile([P, bias_chunks], BF16, name="bias_cols")
        nc.vector.tensor_copy(out=bias_cols[:], in_=bias_cols_ps[:, 0:bias_chunks])
        bias_all = keep.tile([P, 2 * DR], BF16, name="bias_all")
        chunks_per_bank = 8

        def spread_bias(bank, pool, tag, on_scalar):
            spread_ps = pool.tile([P, chunks_per_bank * P], BF16, name="spread_ps", tag=tag)
            for i in range(chunks_per_bank):
                j = bank * chunks_per_bank + i
                nc.tensor.transpose(
                    spread_ps[:, i * P : (i + 1) * P], bias_cols[:, j : j + 1].to_broadcast([P, P]), ident_bf[:]
                )
            cols = slice(bank * chunks_per_bank * P, (bank + 1) * chunks_per_bank * P)
            if on_scalar:
                nc.scalar.copy(out=bias_all[:, cols], in_=spread_ps[:])
            else:
                nc.vector.tensor_copy(out=bias_all[:, cols], in_=spread_ps[:])

        rf_codes = keep.tile([P, RF_PASSES, P], U32, name="rf_codes", align_bytes=64)
        rf_scales = keep.tile([P, RF_PASSES, P], U8, name="rf_scales", align_bytes=64)
        nc.vector.quantize_mx(
            out=rf_codes[:].rearrange("p g b -> p (g b)").bitcast(FP8X4),
            scales=rf_scales[:].rearrange("p g b -> p (g b)"),
            in_=rf_grouped[:].rearrange("p g b t -> p (g b t)"),
        )
        spread_bias(0, psum_main, "main", True)
        spread_bias(1, psum_main, "main", False)
        bbb_row = keep.tile([P, DR], BF16, name="bbb_row")
        nc.vector.memset(bbb_row[:].bitcast(I32), 0)
        ones = keep.tile([P, P], BF16, name="ones")
        nc.vector.memset(ones[:], 1.0)
        nc.scalar.dma_start(out=bbb_row[0:1, :], in_=b_bbrf.rearrange("(r c) -> r c", r=1))

        def product(x_codes, x_scales, w_words, w_planes, passes, bank_by_bank, name):
            banks = []
            for c in range(N_TILES):
                banks.append(psum_main.tile([P, N_TILE], F32, name="%s_%d" % (name, c), tag="main"))
            if bank_by_bank:
                order = [(g, c) for c in range(N_TILES) for g in range(passes)]
            else:
                order = [(g, c) for g in range(passes) for c in range(N_TILES)]
            for g, c in order:
                nc.tensor.matmul_mx(
                    out=banks[c][:],
                    lhsT=x_codes[:, g, :].bitcast(FP8X4),
                    lhsT_scale=x_scales[:, g, :],
                    rhs=w_words[:, g, 2 * c * N_TILE : 2 * (c + 1) * N_TILE].bitcast(FP4X4),
                    rhs_scale=w_planes[:, g, c * N_TILE : (c + 1) * N_TILE],
                    start=(g == 0),
                    stop=(g == passes - 1),
                )
            return banks

        def tile_cols(c):
            return slice(c * N_TILE, (c + 1) * N_TILE)

        def add_bias_exp_and_n(banks, bias, z, w):
            for c in range(N_TILES + 1):
                if c < N_TILES:
                    cols = tile_cols(c)
                    nc.vector.tensor_tensor(out=z[:, cols], in0=banks[c][:], in1=bias[:, cols], op=ALU.add)
                    nc.scalar.activation(out=w[:, cols], in_=z[:, cols], func=ACT.Exp)
                if c > 0:
                    cols = tile_cols(c - 1)
                    nc.vector.scalar_tensor_tensor(
                        out=w[:, cols], in0=w[:, cols], scalar=2.0, in1=w[:, cols], op0=ALU.add, op1=ALU.mult
                    )

        def finish_term(w, z, rest):
            pieces = [tile_cols(c) for c in range(N_TILES - 1)]
            pieces.append(slice(DR - N_TILE, DR - N_TILE // 2))
            pieces.append(slice(DR - N_TILE // 2, DR))
            for i in range(len(pieces) + 1):
                if i < len(pieces):
                    cols = pieces[i]
                    nc.scalar.activation(
                        out=w[:, cols], in_=w[:, cols], func=ACT.Abs_reciprocal_sqrt, scale=0.5, bias=1.0
                    )
                if i > 0:
                    cols = pieces[i - 1]
                    nc.scalar.activation(out=w[:, cols], in_=w[:, cols], func=ACT.Square)
            for i in range(len(pieces) + 1):
                if i < len(pieces):
                    cols = pieces[i]
                    nc.vector.tensor_tensor(out=w[:, cols], in0=w[:, cols], in1=z[:, cols], op=ALU.mult)
                if i > 0:
                    cols = pieces[i - 1]
                    nc.vector.tensor_tensor(out=w[:, cols], in0=rest[:, cols], in1=w[:, cols], op=ALU.subtract)
                    nc.sync.dma_start(out=out[:, cols], in_=w[:, cols])

        z_rf = keep.tile([P, DR], F32, name="z_rf")
        w_rf = keep.tile([P, DR], F32, name="w_rf")
        rf_banks = product(rf_codes, rf_scales, wrf_words, wrf_planes, RF_PASSES, False, "rf_acc")
        for c in range(N_TILES):
            cols = tile_cols(c)
            nc.vector.tensor_tensor(out=z_rf[:, cols], in0=rf_banks[c][:], in1=bias_all[:, cols], op=ALU.add)
            nc.scalar.activation(out=w_rf[:, cols], in_=z_rf[:, cols], func=ACT.Exp)
        for c in range(N_TILES):
            cols = tile_cols(c)
            nc.vector.tensor_scalar_min(out=w_rf[:, cols], in0=w_rf[:, cols], scalar1=EXP_CAP)
        nc.scalar.activation(out=w_rf[:], in_=w_rf[:], func=ACT.Ln, bias=1.0)
        for c in range(N_TILES):
            cols = tile_cols(c)
            nc.scalar.activation(out=w_rf[:, cols], in_=w_rf[:, cols], func=ACT.Tanh)

        bb_grouped = keep.tile([P, BB_PASSES, P, PACK], BF16, name="bb_grouped", align_bytes=64)
        bb_codes = keep.tile([P, BB_PASSES, P], U32, name="bb_codes", align_bytes=64)
        bb_scales = keep.tile([P, BB_PASSES, P], U8, name="bb_scales", align_bytes=64)
        tiles_per_half = BB_TILES // 2
        half_samples = P // 2

        def spread_b_bbrf(bank):
            bbb_ps = psum_side.tile([P, 2 * N_TILE], BF16, name="bbb_ps", tag="side")
            for i in range(2):
                c = 2 * bank + i
                nc.tensor.matmul(
                    out=bbb_ps[:, i * N_TILE : (i + 1) * N_TILE],
                    lhsT=ones[:],
                    rhs=bbb_row[:, c * N_TILE : (c + 1) * N_TILE],
                    start=True,
                    stop=True,
                )
            nc.scalar.copy(out=bias_all[:, DR + 2 * bank * N_TILE : DR + 2 * (bank + 1) * N_TILE], in_=bbb_ps[:])

        for half in range(2):
            mean_t_ps = []
            for g in range(BB_PASSES):
                mean_t_ps.append(psum_side.tile([P, PACK, half_samples], F32, name="mean_t_ps_%d" % g, tag="side"))
            for j_in in range(tiles_per_half):
                j = half * tiles_per_half + j_in
                if j == BB_TILES - 1:
                    spread_b_bbrf(0)
                for g in range(BB_PASSES):
                    for t in range(PACK):
                        for i in range(GROUPS_PER_ROW):
                            nc.tensor.matmul(
                                out=mean_t_ps[g][:, t, j_in * SAMPLES_PER_TILE : (j_in + 1) * SAMPLES_PER_TILE],
                                lhsT=bb_sb[:, j, i, g * K_PASS + t : (g + 1) * K_PASS : PACK],
                                rhs=group_mean[:],
                                start=(i == 0),
                                stop=(i == GROUPS_PER_ROW - 1),
                            )
            samples = slice(half * half_samples, (half + 1) * half_samples)
            for g in range(BB_PASSES):
                nc.vector.tensor_copy(
                    out=bb_grouped[:, g, samples, :], in_=mean_t_ps[g][:].rearrange("p t b -> p b t")
                )
            for g in range(BB_PASSES):
                nc.vector.quantize_mx(
                    out=bb_codes[:, g, samples].bitcast(FP8X4),
                    scales=bb_scales[:, g, samples],
                    in_=bb_grouped[:, g, samples, :].rearrange("p b t -> p (b t)"),
                )
        spread_b_bbrf(1)

        for c in range(N_TILES):
            cols = tile_cols(c)
            nc.vector.tensor_tensor(out=w_rf[:, cols], in0=w_rf[:, cols], in1=z_rf[:, cols], op=ALU.mult)

        z_bb = keep.tile([P, DR], F32, name="z_bb")
        w_bb = keep.tile([P, DR], F32, name="w_bb")
        bb_banks = product(bb_codes, bb_scales, wbb_words, wbb_planes, BB_PASSES, True, "bb_acc")
        add_bias_exp_and_n(bb_banks, bias_all[:, DR : 2 * DR], z_bb, w_bb)
        for c in range(N_TILES):
            cols = tile_cols(c)
            nc.vector.tensor_tensor(out=w_rf[:, cols], in0=w_rf[:, cols], in1=z_bb[:, cols], op=ALU.add)
        finish_term(w_bb, z_bb, w_rf)
